import numpy as np
import ml_dtypes


def mxq(x, axis, fmt="e4m3"):
    dtype, down = {"e4m3": (ml_dtypes.float8_e4m3fn, 7), "e5m2": (ml_dtypes.float8_e5m2, 14)}[fmt]
    v = np.moveaxis(np.asarray(x, np.float32).astype(ml_dtypes.bfloat16).astype(np.float64), axis, -1)
    blocks = v.reshape(v.shape[:-1] + (-1, 32))
    amax = np.abs(blocks).max(-1, keepdims=True)
    byte = np.maximum(np.where(amax > 0, np.frexp(amax)[1] - 1 + 127, 0) - down, 1)
    scale = np.exp2(byte - 127.0)
    codes = (blocks / scale).astype(np.float32).astype(dtype).astype(np.float64)
    return np.moveaxis((codes * scale).reshape(v.shape), -1, axis)


WIDE = False


def mx_kscale(k):
    if not WIDE:
        return np.ones(k)
    levels = np.array([10, -10, 5, -5, 0])
    a = np.random.permutation(np.resize(levels, k // 512 * 4)).reshape(k // 512, 4)
    idx = np.arange(k)
    return np.exp2(a[idx // 512, idx % 128 // 32])


BF16 = ml_dtypes.bfloat16


def bf(x):
    return np.asarray(x, np.float32).astype(BF16)


def f64(x):
    return np.asarray(x).astype(np.float64)


T, B, D_IN, D_H, D_K, D_OUT = 8, 256, 512, 1024, 1024, 256


def setup_inputs():
    s, t = mx_kscale(D_H), mx_kscale(D_K)
    return {"h1": bf(np.maximum(np.random.standard_normal((T, B, D_H)), 0.0) * s),
            "W2": bf(np.random.standard_normal((T, D_H, D_K)) * 1.4 / np.sqrt(D_H) / s[:, None] * t),
            "b2": bf(np.random.standard_normal((T, D_K)) * 0.2 * t),
            "W3": bf(np.random.standard_normal((T, D_K, D_OUT)) * 1.4 / np.sqrt(D_K) / t[:, None]),
            "b3": bf(np.random.standard_normal((T, D_OUT)) * 0.2)}


def reference(h1, W2, b2, W3, b3):
    h2 = np.maximum((mxq(f64(h1), 2, "e4m3") @ mxq(f64(W2), 1, "e4m3")) + f64(b2)[:, None, :], 0.0)
    out = (mxq(h2, 2, "e4m3") @ mxq(f64(W3), 1, "e4m3")) + f64(b3)[:, None, :]
    return out.mean(axis=0)

@@ -1,0 +1,320 @@
+from contextlib import ExitStack
+
+import concourse.mybir as mybir
+from concourse.masks import make_identity
+
+BF16 = mybir.dt.bfloat16
+F32 = mybir.dt.float32
+U32 = mybir.dt.uint32
+U8 = mybir.dt.uint8
+FP8X4 = mybir.dt.float8_e4m3fn_x4
+RELU = mybir.ActivationFunctionType.Relu
+MULT = mybir.AluOpType.mult
+ADD = mybir.AluOpType.add
+
+TREES, BATCH, D_H, D_K, D_OUT = 8, 256, 1024, 1024, 256
+FLOPS = 2 * TREES * BATCH * (D_H * D_K + D_K * D_OUT)
+
+P = 128
+PACK = 4
+K_PASS = P * PACK
+PASSES = D_H // K_PASS
+B_TILES = BATCH // P
+CHUNKS = K_PASS // P
+
+UNIT_COLS = K_PASS
+HALVES = D_K // UNIT_COLS
+UNITS_PER_TREE = PASSES * HALVES
+UNITS = TREES * UNITS_PER_TREE
+
+SCALAR_COLS = 272
+
+RUN = 4
+RAW_TREES = 4
+
+
+def regroup(copy, grouped, rows):
+    copy(
+        out=grouped.rearrange("p (c i j) -> p c j i", i=RUN, j=PACK),
+        in_=rows.rearrange("p j (c i) -> p c j i", i=RUN),
+    )
+
+
+def tile_randomforestmlp_pa_kernel(tc, h1, W2, b2, W3, b3, out):
+    nc = tc.nc
+    with ExitStack() as ctx:
+        const = ctx.enter_context(tc.tile_pool(name="const", bufs=1))
+        raw = ctx.enter_context(tc.tile_pool(name="raw", bufs=RAW_TREES))
+        w2_stage = ctx.enter_context(tc.tile_pool(name="w2_stage", bufs=4))
+        w2_mx = ctx.enter_context(tc.tile_pool(name="w2_mx", bufs=6))
+        per_tree = ctx.enter_context(tc.tile_pool(name="per_tree", bufs=2))
+        per_half = ctx.enter_context(tc.tile_pool(name="per_half", bufs=3))
+        acc_psum = ctx.enter_context(tc.psum_pool(name="acc_psum", bufs=1))
+        tr_psum = ctx.enter_context(tc.psum_pool(name="tr_psum", bufs=2))
+        h2_psum = ctx.enter_context(tc.psum_pool(name="h2_psum", bufs=4))
+        ctx.enter_context(tc.manual_schedule())
+
+        h1_raw, w2_raw, w3_raw = {}, {}, {}
+        h1_banks, h1_grouped, h1_mx = {}, {}, {}
+        w2_grouped, w2_units = {}, {}
+        w3_grouped, w3_mx = {}, {}
+        h2_banks, h2_plain, h2_grouped, h2_mx = {}, {}, {}, {}
+
+        def live(t):
+            return 0 <= t < TREES
+
+        def load_h1(t):
+            if not live(t):
+                return
+            h1_raw[t] = raw.tile([P, B_TILES * D_H], BF16, name="h1_raw")
+            nc.sync.dma_start(
+                out=h1_raw[t][:], in_=h1[t].rearrange("(p r) k -> p (r k)", r=B_TILES)
+            )
+
+        def load_w2(t, g):
+            if not live(t):
+                return
+            w2_raw[t, g] = raw.tile([P, PACK * D_K], BF16, name="w2_raw%d" % g)
+            rows = W2[t, g * K_PASS : (g + 1) * K_PASS, :]
+            nc.sync.dma_start(
+                out=w2_raw[t, g][:], in_=rows.rearrange("(p j) n -> p (j n)", j=PACK)
+            )
+
+        def load_w3(t):
+            if not live(t):
+                return
+            w3_raw[t] = raw.tile([P, PASSES * PACK * D_OUT], BF16, name="w3_raw")
+            nc.sync.dma_start(
+                out=w3_raw[t][:].rearrange("p (c n) -> p c n", n=D_OUT),
+                in_=W3[t].rearrange("(c p) n -> p c n", p=P),
+            )
+
+        def transpose_h1(t):
+            if not live(t):
+                return
+            words = h1_raw[t][:].bitcast(F32).rearrange(
+                "p (r g w u) -> p r g u w", r=B_TILES, g=PASSES, u=2
+            )
+            for g in range(PASSES):
+                h1_banks[t, g] = tr_psum.tile([P, 2, BATCH], F32, name="h1_bank", tag="tr")
+                for u in range(2):
+                    for r in range(B_TILES):
+                        nc.tensor.transpose(
+                            h1_banks[t, g][:, u, r * P : (r + 1) * P],
+                            words[:, r, g, u, :],
+                            identity[:],
+                        )
+            load_h1(t + RAW_TREES)
+
+        def exit_h1(t, g):
+            if not live(t):
+                return
+            if g == 0:
+                h1_grouped[t] = per_tree.tile(
+                    [P, PASSES * PACK * BATCH], BF16, name="h1_grouped", align_bytes=64
+                )
+            one_pass = h1_grouped[t][:, g * PACK * BATCH : (g + 1) * PACK * BATCH]
+            nc.scalar.copy(
+                out=one_pass.bitcast(F32).rearrange("p (b u) -> p b u", u=2),
+                in_=h1_banks[t, g][:].rearrange("p u b -> p b u"),
+            )
+
+        def quantise(pool, name, grouped, width):
+            codes = pool.tile([P, width], U32, name=name + "_codes", align_bytes=64)
+            scales = pool.tile([P, width], U8, name=name + "_scales", align_bytes=64)
+            nc.vector.quantize_mx(out=codes[:].bitcast(FP8X4), scales=scales[:], in_=grouped[:])
+            return codes, scales
+
+        def quantise_h1(t):
+            if live(t):
+                h1_mx[t] = quantise(per_tree, "h1", h1_grouped[t], PASSES * BATCH)
+
+        def regroup_w2(unit):
+            if not 0 <= unit < UNITS:
+                return
+            t, rest = divmod(unit, UNITS_PER_TREE)
+            g, half = divmod(rest, HALVES)
+            w2_grouped[unit] = w2_stage.tile(
+                [P, PACK * UNIT_COLS], BF16, name="w2_grouped", align_bytes=64
+            )
+            rows = w2_raw[t, g][:].rearrange("p (j n) -> p j n", j=PACK)
+            rows = rows[:, :, half * UNIT_COLS : (half + 1) * UNIT_COLS]
+            split = PACK * SCALAR_COLS
+            regroup(nc.scalar.copy, w2_grouped[unit][:, :split], rows[:, :, :SCALAR_COLS])
+            regroup(nc.vector.tensor_copy, w2_grouped[unit][:, split:], rows[:, :, SCALAR_COLS:])
+            if half == HALVES - 1:
+                load_w2(t + RAW_TREES, g)
+
+        def quantise_w2(unit):
+            if 0 <= unit < UNITS:
+                w2_units[unit] = quantise(w2_mx, "w2", w2_grouped[unit], UNIT_COLS)
+
+        def w2_slot(unit):
+            regroup_w2(unit + 1)
+            quantise_w2(unit)
+
+        def regroup_w3(t, g):
+            if not live(t):
+                return
+            if g == 0:
+                w3_grouped[t] = per_tree.tile(
+                    [P, PASSES * PACK * D_OUT], BF16, name="w3_grouped", align_bytes=64
+                )
+            cols = slice(g * PACK * D_OUT, (g + 1) * PACK * D_OUT)
+            regroup(
+                nc.vector.tensor_copy,
+                w3_grouped[t][:, cols],
+                w3_raw[t][:, cols].rearrange("p (j n) -> p j n", j=PACK),
+            )
+            if g == PASSES - 1:
+                load_w3(t + RAW_TREES)
+
+        def quantise_w3(t):
+            if live(t):
+                w3_mx[t] = quantise(per_tree, "w3", w3_grouped[t], PASSES * D_OUT)
+
+        def stage1(t, half):
+            if not live(t):
+                return
+            h1_codes, h1_scales = h1_mx[t]
+            for c in range(CHUNKS):
+                if c % 2 == 0:
+                    bank = h2_psum.tile([P, 2, BATCH], F32, name="h2_bank")
+                    h2_banks[t, half, c // 2] = bank
+                m_cols = slice(c * P, (c + 1) * P)
+                for g in range(PASSES):
+                    w2_codes, w2_scales = w2_units[(t * PASSES + g) * HALVES + half]
+                    b_cols = slice(g * BATCH, (g + 1) * BATCH)
+                    nc.tensor.matmul_mx(
+                        out=bank[:, c % 2, :],
+                        lhsT=w2_codes[:, m_cols].bitcast(FP8X4),
+                        lhsT_scale=w2_scales[:, m_cols],
+                        rhs=h1_codes[:, b_cols].bitcast(FP8X4),
+                        rhs_scale=h1_scales[:, b_cols],
+                        start=(g == 0),
+                        stop=(g == PASSES - 1),
+                    )
+
+        def exit_h2(t, half):
+            if not live(t):
+                return
+            h2_plain[t, half] = per_half.tile([P, CHUNKS * BATCH], BF16, name="h2_plain")
+            for c in range(CHUNKS):
+                column = (t * HALVES + half) * CHUNKS + c
+                nc.scalar.activation(
+                    out=h2_plain[t, half][:, c * BATCH : (c + 1) * BATCH],
+                    in_=h2_banks[t, half, c // 2][:, c % 2, :],
+                    func=RELU,
+                    bias=b2_columns[:, column : column + 1],
+                    scale=1.0,
+                )
+
+        def regroup_h2(t, half):
+            if not live(t):
+                return
+            h2_grouped[t, half] = per_half.tile(
+                [P, PACK * BATCH], BF16, name="h2_grouped", align_bytes=64
+            )
+            regroup(
+                nc.vector.tensor_copy,
+                h2_grouped[t, half][:],
+                h2_plain[t, half][:].rearrange("p (j b) -> p j b", j=PACK),
+            )
+
+        def quantise_h2(t, half):
+            if live(t):
+                h2_mx[t, half] = quantise(per_half, "h2", h2_grouped[t, half], BATCH)
+
+        def stage2(t, g):
+            if not live(t):
+                return
+            h2_codes, h2_scales = h2_mx[t, g]
+            w3_codes, w3_scales = w3_mx[t]
+            n_cols = slice(g * D_OUT, (g + 1) * D_OUT)
+            for r in range(B_TILES):
+                m_cols = slice(r * P, (r + 1) * P)
+                nc.tensor.matmul_mx(
+                    out=acc[r][:],
+                    lhsT=h2_codes[:, m_cols].bitcast(FP8X4),
+                    lhsT_scale=h2_scales[:, m_cols],
+                    rhs=w3_codes[:, n_cols].bitcast(FP8X4),
+                    rhs_scale=w3_scales[:, n_cols],
+                    start=(t == 0 and g == 0),
+                    stop=(t == TREES - 1 and g == PASSES - 1),
+                )
+
+        b2_rows = const.tile([P, P], BF16, name="b2_rows")
+        b3_rows = const.tile([P, D_OUT], BF16, name="b3_rows")
+        ones = const.tile([P, P], BF16, name="ones")
+        nc.vector.memset(b2_rows[:], 0.0)
+        nc.vector.memset(b3_rows[:], 0.0)
+        nc.vector.memset(ones[:], 1.0)
+        nc.scalar.dma_start(
+            out=b2_rows[: TREES * D_K // P, :], in_=b2.rearrange("t (c p) -> (t c) p", p=P)
+        )
+        nc.scalar.dma_start(out=b3_rows[:TREES, :], in_=b3)
+        for t in range(RAW_TREES):
+            load_h1(t)
+            for g in range(PASSES):
+                load_w2(t, g)
+            load_w3(t)
+        identity = const.tile([P, P], F32, name="identity")
+        make_identity(nc, identity[:])
+        acc = [acc_psum.tile([P, D_OUT], F32, name="acc%d" % r) for r in range(B_TILES)]
+
+        transpose_h1(0)
+        exit_h1(0, 0)
+        exit_h1(0, 1)
+
+        b2_rows_f32 = const.tile([P, P], F32, name="b2_rows_f32")
+        nc.vector.tensor_copy(out=b2_rows_f32[:], in_=b2_rows[:])
+        b2_bank = tr_psum.tile([P, 2, BATCH], F32, name="b2_bank", tag="tr")
+        nc.tensor.transpose(b2_bank[:, 0, :P], b2_rows_f32[:], identity[:])
+        b2_columns = const.tile([P, TREES * D_K // P], F32, name="b2_columns")
+        nc.vector.tensor_copy(out=b2_columns[:], in_=b2_bank[:, 0, : TREES * D_K // P])
+        b3_bank = tr_psum.tile([P, 2, BATCH], F32, name="b3_bank", tag="tr")
+        nc.tensor.matmul(out=b3_bank[:, 0, :], lhsT=ones[:], rhs=b3_rows[:], start=True, stop=True)
+        b3_mean = const.tile([P, D_OUT], F32, name="b3_mean")
+        nc.scalar.mul(out=b3_mean[:], in_=b3_bank[:, 0, :], mul=1.0 / TREES)
+
+        quantise_h1(0)
+        regroup_w2(0)
+
+        for t in range(TREES + 1):
+            first = t * UNITS_PER_TREE
+            w2_slot(first)
+            exit_h2(t - 1, 1)
+            regroup_h2(t - 1, 0)
+            regroup_w3(t, 0)
+
+            w2_slot(first + 1)
+            transpose_h1(t + 1)
+            exit_h1(t + 1, 0)
+            quantise_h2(t - 1, 0)
+            stage2(t - 1, 0)
+            regroup_h2(t - 1, 1)
+
+            w2_slot(first + 2)
+            stage1(t, 0)
+            exit_h1(t + 1, 1)
+            quantise_h2(t - 1, 1)
+            stage2(t - 1, 1)
+            regroup_w3(t, 1)
+
+            w2_slot(first + 3)
+            stage1(t, 1)
+            exit_h2(t, 0)
+            quantise_w3(t)
+            quantise_h1(t + 1)
+
+        out_rows = const.tile([P, B_TILES, D_OUT], F32, name="out_rows")
+        for r in range(B_TILES):
+            nc.vector.scalar_tensor_tensor(
+                out=out_rows[:, r, :],
+                in0=acc[r][:],
+                scalar=1.0 / TREES,
+                in1=b3_mean[:],
+                op0=MULT,
+                op1=ADD,
+            )
+        nc.sync.dma_start(out=out.rearrange("(p r) n -> p r n", r=B_TILES), in_=out_rows[:])

@@ -27,8 +27,9 @@ HALVES = D_K // UNIT_COLS
 UNITS_PER_TREE = PASSES * HALVES
 UNITS = TREES * UNITS_PER_TREE
 
-SCALAR_COLS = 272
+SCALAR_COLS = 304
 
+LEAD = 2
 RUN = 4
 RAW_TREES = 4
 
@@ -45,7 +46,7 @@ def tile_randomforestmlp_pa_kernel(tc, h1, W2, b2, W3, b3, out):
     with ExitStack() as ctx:
         const = ctx.enter_context(tc.tile_pool(name="const", bufs=1))
         raw = ctx.enter_context(tc.tile_pool(name="raw", bufs=RAW_TREES))
-        w2_stage = ctx.enter_context(tc.tile_pool(name="w2_stage", bufs=4))
+        w2_stage = ctx.enter_context(tc.tile_pool(name="w2_stage", bufs=LEAD + 3))
         w2_mx = ctx.enter_context(tc.tile_pool(name="w2_mx", bufs=6))
         per_tree = ctx.enter_context(tc.tile_pool(name="per_tree", bufs=2))
         per_half = ctx.enter_context(tc.tile_pool(name="per_half", bufs=3))
@@ -75,10 +76,12 @@ def tile_randomforestmlp_pa_kernel(tc, h1, W2, b2, W3, b3, out):
             if not live(t):
                 return
             w2_raw[t, g] = raw.tile([P, PACK * D_K], BF16, name="w2_raw%d" % g)
-            rows = W2[t, g * K_PASS : (g + 1) * K_PASS, :]
-            nc.sync.dma_start(
-                out=w2_raw[t, g][:], in_=rows.rearrange("(p j) n -> p (j n)", j=PACK)
-            )
+            rows = W2[t, g * K_PASS : (g + 1) * K_PASS, :].rearrange("(p j) n -> p j n", j=PACK)
+            tile_rows = w2_raw[t, g][:].rearrange("p (j n) -> p j n", j=PACK)
+            pieces = HALVES if (t, g) == (0, 0) else 1
+            for piece in range(pieces):
+                cols = slice(piece * D_K // pieces, (piece + 1) * D_K // pieces)
+                nc.sync.dma_start(out=tile_rows[:, :, cols], in_=rows[:, :, cols])
 
         def load_w3(t):
             if not live(t):
@@ -150,7 +153,7 @@ def tile_randomforestmlp_pa_kernel(tc, h1, W2, b2, W3, b3, out):
                 w2_units[unit] = quantise(w2_mx, "w2", w2_grouped[unit], UNIT_COLS)
 
         def w2_slot(unit):
-            regroup_w2(unit + 1)
+            regroup_w2(unit + LEAD)
             quantise_w2(unit)
 
         def regroup_w3(t, g):
@@ -249,22 +252,18 @@ def tile_randomforestmlp_pa_kernel(tc, h1, W2, b2, W3, b3, out):
         nc.vector.memset(b2_rows[:], 0.0)
         nc.vector.memset(b3_rows[:], 0.0)
         nc.vector.memset(ones[:], 1.0)
-        nc.scalar.dma_start(
+        nc.sync.dma_start(
             out=b2_rows[: TREES * D_K // P, :], in_=b2.rearrange("t (c p) -> (t c) p", p=P)
         )
-        nc.scalar.dma_start(out=b3_rows[:TREES, :], in_=b3)
+        nc.sync.dma_start(out=b3_rows[:TREES, :], in_=b3)
         for t in range(RAW_TREES):
+            load_w2(t, 0)
             load_h1(t)
-            for g in range(PASSES):
-                load_w2(t, g)
+            load_w2(t, 1)
             load_w3(t)
         identity = const.tile([P, P], F32, name="identity")
         make_identity(nc, identity[:])
         acc = [acc_psum.tile([P, D_OUT], F32, name="acc%d" % r) for r in range(B_TILES)]
-
-        transpose_h1(0)
-        exit_h1(0, 0)
-        exit_h1(0, 1)
 
         b2_rows_f32 = const.tile([P, P], F32, name="b2_rows_f32")
         nc.vector.tensor_copy(out=b2_rows_f32[:], in_=b2_rows[:])
@@ -277,35 +276,32 @@ def tile_randomforestmlp_pa_kernel(tc, h1, W2, b2, W3, b3, out):
         b3_mean = const.tile([P, D_OUT], F32, name="b3_mean")
         nc.scalar.mul(out=b3_mean[:], in_=b3_bank[:, 0, :], mul=1.0 / TREES)
 
-        quantise_h1(0)
-        regroup_w2(0)
-
-        for t in range(TREES + 1):
+        for t in range(-1, TREES + 1):
             first = t * UNITS_PER_TREE
             w2_slot(first)
-            exit_h2(t - 1, 1)
-            regroup_h2(t - 1, 0)
+            exit_h2(t - 1, 0)
+            quantise_h1(t)
             regroup_w3(t, 0)
 
             w2_slot(first + 1)
             transpose_h1(t + 1)
+            exit_h2(t - 1, 1)
+            regroup_h2(t - 1, 0)
+            regroup_w3(t, 1)
+
+            w2_slot(first + 2)
+            stage1(t, 0)
             exit_h1(t + 1, 0)
             quantise_h2(t - 1, 0)
             stage2(t - 1, 0)
             regroup_h2(t - 1, 1)
 
-            w2_slot(first + 2)
-            stage1(t, 0)
+            w2_slot(first + 3)
+            stage1(t, 1)
             exit_h1(t + 1, 1)
             quantise_h2(t - 1, 1)
             stage2(t - 1, 1)
-            regroup_w3(t, 1)
-
-            w2_slot(first + 3)
-            stage1(t, 1)
-            exit_h2(t, 0)
             quantise_w3(t)
-            quantise_h1(t + 1)
 
         out_rows = const.tile([P, B_TILES, D_OUT], F32, name="out_rows")
         for r in range(B_TILES):

@@ -27,7 +27,7 @@ HALVES = D_K // UNIT_COLS
 UNITS_PER_TREE = PASSES * HALVES
 UNITS = TREES * UNITS_PER_TREE
 
-SCALAR_COLS = 304
+SCALAR_COLS = 256
 
 LEAD = 2
 RUN = 4

from contextlib import ExitStack

import concourse.mybir as mybir
from concourse.masks import make_identity

BF16 = mybir.dt.bfloat16
F32 = mybir.dt.float32
U32 = mybir.dt.uint32
U8 = mybir.dt.uint8
FP8X4 = mybir.dt.float8_e4m3fn_x4
RELU = mybir.ActivationFunctionType.Relu
MULT = mybir.AluOpType.mult
ADD = mybir.AluOpType.add

TREES, BATCH, D_H, D_K, D_OUT = 8, 256, 1024, 1024, 256
FLOPS = 2 * TREES * BATCH * (D_H * D_K + D_K * D_OUT)

P = 128
PACK = 4
K_PASS = P * PACK
PASSES = D_H // K_PASS
B_TILES = BATCH // P
CHUNKS = K_PASS // P

UNIT_COLS = K_PASS
HALVES = D_K // UNIT_COLS
UNITS_PER_TREE = PASSES * HALVES
UNITS = TREES * UNITS_PER_TREE

SCALAR_COLS = 256

LEAD = 2
RUN = 4
RAW_TREES = 4


def regroup(copy, grouped, rows):
    copy(
        out=grouped.rearrange("p (c i j) -> p c j i", i=RUN, j=PACK),
        in_=rows.rearrange("p j (c i) -> p c j i", i=RUN),
    )


def tile_randomforestmlp_pa_kernel(tc, h1, W2, b2, W3, b3, out):
    nc = tc.nc
    with ExitStack() as ctx:
        const = ctx.enter_context(tc.tile_pool(name="const", bufs=1))
        raw = ctx.enter_context(tc.tile_pool(name="raw", bufs=RAW_TREES))
        w2_stage = ctx.enter_context(tc.tile_pool(name="w2_stage", bufs=LEAD + 3))
        w2_mx = ctx.enter_context(tc.tile_pool(name="w2_mx", bufs=6))
        per_tree = ctx.enter_context(tc.tile_pool(name="per_tree", bufs=2))
        per_half = ctx.enter_context(tc.tile_pool(name="per_half", bufs=3))
        acc_psum = ctx.enter_context(tc.psum_pool(name="acc_psum", bufs=1))
        tr_psum = ctx.enter_context(tc.psum_pool(name="tr_psum", bufs=2))
        h2_psum = ctx.enter_context(tc.psum_pool(name="h2_psum", bufs=4))
        ctx.enter_context(tc.manual_schedule())

        h1_raw, w2_raw, w3_raw = {}, {}, {}
        h1_banks, h1_grouped, h1_mx = {}, {}, {}
        w2_grouped, w2_units = {}, {}
        w3_grouped, w3_mx = {}, {}
        h2_banks, h2_plain, h2_grouped, h2_mx = {}, {}, {}, {}

        def live(t):
            return 0 <= t < TREES

        def load_h1(t):
            if not live(t):
                return
            h1_raw[t] = raw.tile([P, B_TILES * D_H], BF16, name="h1_raw")
            nc.sync.dma_start(
                out=h1_raw[t][:], in_=h1[t].rearrange("(p r) k -> p (r k)", r=B_TILES)
            )

        def load_w2(t, g):
            if not live(t):
                return
            w2_raw[t, g] = raw.tile([P, PACK * D_K], BF16, name="w2_raw%d" % g)
            rows = W2[t, g * K_PASS : (g + 1) * K_PASS, :].rearrange("(p j) n -> p j n", j=PACK)
            tile_rows = w2_raw[t, g][:].rearrange("p (j n) -> p j n", j=PACK)
            pieces = HALVES if (t, g) == (0, 0) else 1
            for piece in range(pieces):
                cols = slice(piece * D_K // pieces, (piece + 1) * D_K // pieces)
                nc.sync.dma_start(out=tile_rows[:, :, cols], in_=rows[:, :, cols])

        def load_w3(t):
            if not live(t):
                return
            w3_raw[t] = raw.tile([P, PASSES * PACK * D_OUT], BF16, name="w3_raw")
            nc.sync.dma_start(
                out=w3_raw[t][:].rearrange("p (c n) -> p c n", n=D_OUT),
                in_=W3[t].rearrange("(c p) n -> p c n", p=P),
            )

        def transpose_h1(t):
            if not live(t):
                return
            words = h1_raw[t][:].bitcast(F32).rearrange(
                "p (r g w u) -> p r g u w", r=B_TILES, g=PASSES, u=2
            )
            for g in range(PASSES):
                h1_banks[t, g] = tr_psum.tile([P, 2, BATCH], F32, name="h1_bank", tag="tr")
                for u in range(2):
                    for r in range(B_TILES):
                        nc.tensor.transpose(
                            h1_banks[t, g][:, u, r * P : (r + 1) * P],
                            words[:, r, g, u, :],
                            identity[:],
                        )
            load_h1(t + RAW_TREES)

        def exit_h1(t, g):
            if not live(t):
                return
            if g == 0:
                h1_grouped[t] = per_tree.tile(
                    [P, PASSES * PACK * BATCH], BF16, name="h1_grouped", align_bytes=64
                )
            one_pass = h1_grouped[t][:, g * PACK * BATCH : (g + 1) * PACK * BATCH]
            nc.scalar.copy(
                out=one_pass.bitcast(F32).rearrange("p (b u) -> p b u", u=2),
                in_=h1_banks[t, g][:].rearrange("p u b -> p b u"),
            )

        def quantise(pool, name, grouped, width):
            codes = pool.tile([P, width], U32, name=name + "_codes", align_bytes=64)
            scales = pool.tile([P, width], U8, name=name + "_scales", align_bytes=64)
            nc.vector.quantize_mx(out=codes[:].bitcast(FP8X4), scales=scales[:], in_=grouped[:])
            return codes, scales

        def quantise_h1(t):
            if live(t):
                h1_mx[t] = quantise(per_tree, "h1", h1_grouped[t], PASSES * BATCH)

        def regroup_w2(unit):
            if not 0 <= unit < UNITS:
                return
            t, rest = divmod(unit, UNITS_PER_TREE)
            g, half = divmod(rest, HALVES)
            w2_grouped[unit] = w2_stage.tile(
                [P, PACK * UNIT_COLS], BF16, name="w2_grouped", align_bytes=64
            )
            rows = w2_raw[t, g][:].rearrange("p (j n) -> p j n", j=PACK)
            rows = rows[:, :, half * UNIT_COLS : (half + 1) * UNIT_COLS]
            split = PACK * SCALAR_COLS
            regroup(nc.scalar.copy, w2_grouped[unit][:, :split], rows[:, :, :SCALAR_COLS])
            regroup(nc.vector.tensor_copy, w2_grouped[unit][:, split:], rows[:, :, SCALAR_COLS:])
            if half == HALVES - 1:
                load_w2(t + RAW_TREES, g)

        def quantise_w2(unit):
            if 0 <= unit < UNITS:
                w2_units[unit] = quantise(w2_mx, "w2", w2_grouped[unit], UNIT_COLS)

        def w2_slot(unit):
            regroup_w2(unit + LEAD)
            quantise_w2(unit)

        def regroup_w3(t, g):
            if not live(t):
                return
            if g == 0:
                w3_grouped[t] = per_tree.tile(
                    [P, PASSES * PACK * D_OUT], BF16, name="w3_grouped", align_bytes=64
                )
            cols = slice(g * PACK * D_OUT, (g + 1) * PACK * D_OUT)
            regroup(
                nc.vector.tensor_copy,
                w3_grouped[t][:, cols],
                w3_raw[t][:, cols].rearrange("p (j n) -> p j n", j=PACK),
            )
            if g == PASSES - 1:
                load_w3(t + RAW_TREES)

        def quantise_w3(t):
            if live(t):
                w3_mx[t] = quantise(per_tree, "w3", w3_grouped[t], PASSES * D_OUT)

        def stage1(t, half):
            if not live(t):
                return
            h1_codes, h1_scales = h1_mx[t]
            for c in range(CHUNKS):
                if c % 2 == 0:
                    bank = h2_psum.tile([P, 2, BATCH], F32, name="h2_bank")
                    h2_banks[t, half, c // 2] = bank
                m_cols = slice(c * P, (c + 1) * P)
                for g in range(PASSES):
                    w2_codes, w2_scales = w2_units[(t * PASSES + g) * HALVES + half]
                    b_cols = slice(g * BATCH, (g + 1) * BATCH)
                    nc.tensor.matmul_mx(
                        out=bank[:, c % 2, :],
                        lhsT=w2_codes[:, m_cols].bitcast(FP8X4),
                        lhsT_scale=w2_scales[:, m_cols],
                        rhs=h1_codes[:, b_cols].bitcast(FP8X4),
                        rhs_scale=h1_scales[:, b_cols],
                        start=(g == 0),
                        stop=(g == PASSES - 1),
                    )

        def exit_h2(t, half):
            if not live(t):
                return
            h2_plain[t, half] = per_half.tile([P, CHUNKS * BATCH], BF16, name="h2_plain")
            for c in range(CHUNKS):
                column = (t * HALVES + half) * CHUNKS + c
                nc.scalar.activation(
                    out=h2_plain[t, half][:, c * BATCH : (c + 1) * BATCH],
                    in_=h2_banks[t, half, c // 2][:, c % 2, :],
                    func=RELU,
                    bias=b2_columns[:, column : column + 1],
                    scale=1.0,
                )

        def regroup_h2(t, half):
            if not live(t):
                return
            h2_grouped[t, half] = per_half.tile(
                [P, PACK * BATCH], BF16, name="h2_grouped", align_bytes=64
            )
            regroup(
                nc.vector.tensor_copy,
                h2_grouped[t, half][:],
                h2_plain[t, half][:].rearrange("p (j b) -> p j b", j=PACK),
            )

        def quantise_h2(t, half):
            if live(t):
                h2_mx[t, half] = quantise(per_half, "h2", h2_grouped[t, half], BATCH)

        def stage2(t, g):
            if not live(t):
                return
            h2_codes, h2_scales = h2_mx[t, g]
            w3_codes, w3_scales = w3_mx[t]
            n_cols = slice(g * D_OUT, (g + 1) * D_OUT)
            for r in range(B_TILES):
                m_cols = slice(r * P, (r + 1) * P)
                nc.tensor.matmul_mx(
                    out=acc[r][:],
                    lhsT=h2_codes[:, m_cols].bitcast(FP8X4),
                    lhsT_scale=h2_scales[:, m_cols],
                    rhs=w3_codes[:, n_cols].bitcast(FP8X4),
                    rhs_scale=w3_scales[:, n_cols],
                    start=(t == 0 and g == 0),
                    stop=(t == TREES - 1 and g == PASSES - 1),
                )

        b2_rows = const.tile([P, P], BF16, name="b2_rows")
        b3_rows = const.tile([P, D_OUT], BF16, name="b3_rows")
        ones = const.tile([P, P], BF16, name="ones")
        nc.vector.memset(b2_rows[:], 0.0)
        nc.vector.memset(b3_rows[:], 0.0)
        nc.vector.memset(ones[:], 1.0)
        nc.sync.dma_start(
            out=b2_rows[: TREES * D_K // P, :], in_=b2.rearrange("t (c p) -> (t c) p", p=P)
        )
        nc.sync.dma_start(out=b3_rows[:TREES, :], in_=b3)
        for t in range(RAW_TREES):
            load_w2(t, 0)
            load_h1(t)
            load_w2(t, 1)
            load_w3(t)
        identity = const.tile([P, P], F32, name="identity")
        make_identity(nc, identity[:])
        acc = [acc_psum.tile([P, D_OUT], F32, name="acc%d" % r) for r in range(B_TILES)]

        b2_rows_f32 = const.tile([P, P], F32, name="b2_rows_f32")
        nc.vector.tensor_copy(out=b2_rows_f32[:], in_=b2_rows[:])
        b2_bank = tr_psum.tile([P, 2, BATCH], F32, name="b2_bank", tag="tr")
        nc.tensor.transpose(b2_bank[:, 0, :P], b2_rows_f32[:], identity[:])
        b2_columns = const.tile([P, TREES * D_K // P], F32, name="b2_columns")
        nc.vector.tensor_copy(out=b2_columns[:], in_=b2_bank[:, 0, : TREES * D_K // P])
        b3_bank = tr_psum.tile([P, 2, BATCH], F32, name="b3_bank", tag="tr")
        nc.tensor.matmul(out=b3_bank[:, 0, :], lhsT=ones[:], rhs=b3_rows[:], start=True, stop=True)
        b3_mean = const.tile([P, D_OUT], F32, name="b3_mean")
        nc.scalar.mul(out=b3_mean[:], in_=b3_bank[:, 0, :], mul=1.0 / TREES)

        for t in range(-1, TREES + 1):
            first = t * UNITS_PER_TREE
            w2_slot(first)
            exit_h2(t - 1, 0)
            quantise_h1(t)
            regroup_w3(t, 0)

            w2_slot(first + 1)
            transpose_h1(t + 1)
            exit_h2(t - 1, 1)
            regroup_h2(t - 1, 0)
            regroup_w3(t, 1)

            w2_slot(first + 2)
            stage1(t, 0)
            exit_h1(t + 1, 0)
            quantise_h2(t - 1, 0)
            stage2(t - 1, 0)
            regroup_h2(t - 1, 1)

            w2_slot(first + 3)
            stage1(t, 1)
            exit_h1(t + 1, 1)
            quantise_h2(t - 1, 1)
            stage2(t - 1, 1)
            quantise_w3(t)

        out_rows = const.tile([P, B_TILES, D_OUT], F32, name="out_rows")
        for r in range(B_TILES):
            nc.vector.scalar_tensor_tensor(
                out=out_rows[:, r, :],
                in0=acc[r][:],
                scalar=1.0 / TREES,
                in1=b3_mean[:],
                op0=MULT,
                op1=ADD,
            )
        nc.sync.dma_start(out=out.rearrange("(p r) n -> p r n", r=B_TILES), in_=out_rows[:])
